import numpy as np
import ml_dtypes


def mxq(x, axis, fmt="e4m3"):
    dtype, down = {"e4m3": (ml_dtypes.float8_e4m3fn, 7), "e5m2": (ml_dtypes.float8_e5m2, 14)}[fmt]
    v = np.moveaxis(np.asarray(x, np.float32).astype(ml_dtypes.bfloat16).astype(np.float64), axis, -1)
    blocks = v.reshape(v.shape[:-1] + (-1, 32))
    amax = np.abs(blocks).max(-1, keepdims=True)
    byte = np.maximum(np.where(amax > 0, np.frexp(amax)[1] - 1 + 127, 0) - down, 1)
    scale = np.exp2(byte - 127.0)
    codes = (blocks / scale).astype(np.float32).astype(dtype).astype(np.float64)
    return np.moveaxis((codes * scale).reshape(v.shape), -1, axis)


WIDE = False


def mx_kscale(k):
    if not WIDE:
        return np.ones(k)
    levels = np.array([10, -10, 5, -5, 0])
    a = np.random.permutation(np.resize(levels, k // 512 * 4)).reshape(k // 512, 4)
    idx = np.arange(k)
    return np.exp2(a[idx // 512, idx % 128 // 32])


BF16 = ml_dtypes.bfloat16


def bf(x):
    return np.asarray(x, np.float32).astype(BF16)


def f64(x):
    return np.asarray(x).astype(np.float64)


B, T, C, H = 4, 1024, 512, 4
HD = C // H


def rotary_pos_emb(v):
    exponents = f64(np.arange(0, HD, 2)[: HD // 2] // HD)
    freqs = 1.0 / np.power(1000.0, exponents)
    theta = f64(np.arange(T))[:, None] * freqs[None, :]
    cos = np.cos(theta)[None, :, None, :]
    sin = np.sin(theta)[None, :, None, :]
    vr = v.reshape(B, T, H, HD // 2, 2)
    v0, v1 = vr[..., 0], vr[..., 1]
    out = np.stack([v0 * cos - v1 * sin, v0 * sin + v1 * cos], axis=-1)
    return out.reshape(B, T, H, HD)


def setup_inputs():
    s = mx_kscale(C)
    return {"x": bf(np.random.standard_normal((B, T, C)) * s),
            "wq": bf(np.random.standard_normal((C, C)) / np.sqrt(C) / s[None, :]),
            "wk": bf(np.random.standard_normal((C, C)) / np.sqrt(C) / s[None, :])}


def reference(x, wq, wk):
    xm = mxq(f64(x), 2, "e4m3")
    q = (xm @ mxq(f64(wq), 1, "e4m3").T).reshape(B, T, H, HD)
    k = (xm @ mxq(f64(wk), 1, "e4m3").T).reshape(B, T, H, HD)
    return rotary_pos_emb(q), rotary_pos_emb(k)

@@ -1,0 +1,245 @@
+import math
+from contextlib import ExitStack
+
+import concourse.mybir as mybir
+from concourse.masks import make_identity
+
+F32 = mybir.dt.float32
+BF16 = mybir.dt.bfloat16
+U32 = mybir.dt.uint32
+U8 = mybir.dt.uint8
+FP8X4 = mybir.dt.float8_e4m3fn_x4
+ALU = mybir.AluOpType
+ACT = mybir.ActivationFunctionType
+
+P = 128
+BATCH, SEQ, CHANNELS = 4, 1024, 512
+TOKENS = BATCH * SEQ
+PAIRS = CHANNELS // 2
+WORDS = CHANNELS // 2
+TILES_PER_GROUP = 4
+GROUP_TOKENS = P * TILES_PER_GROUP
+GROUPS = TOKENS // GROUP_TOKENS
+GROUPS_PER_SEQ = SEQ // GROUP_TOKENS
+TILES_PER_BANK = 2
+TILES_PER_STORE = 2
+
+FLOPS = 2 * TOKENS * CHANNELS * 2 * CHANNELS
+
+ROUND_TO_WHOLE = 1.5 * 2.0**23
+TWO_PI_HIGH = round(2.0 * math.pi * 2.0**13) / 2.0**13
+TWO_PI_LOW = 2.0 * math.pi - TWO_PI_HIGH
+
+
+def build_cos_sin(nc, consts):
+    columns = GROUPS_PER_SEQ * TILES_PER_GROUP
+    position = consts.tile([P, columns], F32)
+    nc.gpsimd.iota(
+        position[:],
+        pattern=[[GROUP_TOKENS, GROUPS_PER_SEQ], [1, TILES_PER_GROUP]],
+        base=0,
+        channel_multiplier=TILES_PER_GROUP,
+        allow_small_or_imprecise_dtypes=True,
+    )
+    shifted = consts.tile([P, columns], F32)
+    nc.vector.tensor_scalar(
+        out=shifted[:], in0=position[:], scalar1=1.0 / (2.0 * math.pi), scalar2=ROUND_TO_WHOLE,
+        op0=ALU.mult, op1=ALU.add,
+    )
+    turns = consts.tile([P, columns], F32)
+    nc.vector.tensor_scalar(
+        out=turns[:], in0=shifted[:], scalar1=ROUND_TO_WHOLE, scalar2=None, op0=ALU.subtract
+    )
+    coarse = consts.tile([P, columns], F32)
+    nc.vector.scalar_tensor_tensor(
+        out=coarse[:], in0=turns[:], scalar=-TWO_PI_HIGH, in1=position[:], op0=ALU.mult, op1=ALU.add
+    )
+    angle = consts.tile([P, columns], F32)
+    nc.vector.scalar_tensor_tensor(
+        out=angle[:], in0=turns[:], scalar=-TWO_PI_LOW, in1=coarse[:], op0=ALU.mult, op1=ALU.add
+    )
+    magnitude = consts.tile([P, columns], F32)
+    nc.vector.scalar_tensor_tensor(
+        out=magnitude[:], in0=angle[:], scalar=-1.0, in1=angle[:], op0=ALU.mult, op1=ALU.max
+    )
+    sin_half = consts.tile([P, columns], F32)
+    nc.scalar.activation(out=sin_half[:], in_=angle[:], func=ACT.Sin, scale=0.5)
+    complement = consts.tile([P, columns], F32)
+    nc.vector.tensor_scalar(
+        out=complement[:], in0=magnitude[:], scalar1=-0.5, scalar2=math.pi / 2.0,
+        op0=ALU.mult, op1=ALU.add,
+    )
+    cos_half = consts.tile([P, columns], F32)
+    nc.scalar.activation(out=cos_half[:], in_=complement[:], func=ACT.Sin)
+    sin = consts.tile([P, columns], F32)
+    nc.vector.scalar_tensor_tensor(
+        out=sin[:], in0=sin_half[:], scalar=2.0, in1=cos_half[:], op0=ALU.mult, op1=ALU.mult
+    )
+    cos_less_one = consts.tile([P, columns], F32)
+    nc.vector.scalar_tensor_tensor(
+        out=cos_less_one[:], in0=sin_half[:], scalar=-2.0, in1=sin_half[:], op0=ALU.mult, op1=ALU.mult
+    )
+    cos = consts.tile([P, columns], F32)
+    nc.vector.tensor_scalar(
+        out=cos[:], in0=cos_less_one[:], scalar1=1.0, scalar2=None, op0=ALU.add
+    )
+    neg_cos = consts.tile([P, columns], F32)
+    nc.vector.tensor_scalar(
+        out=neg_cos[:], in0=cos_less_one[:], scalar1=-1.0, scalar2=-1.0, op0=ALU.mult, op1=ALU.add
+    )
+    return cos, neg_cos, sin
+
+
+def tile_attention_pa_t_kernel(tc, x, wq, wk, out_0, out_1):
+    nc = tc.nc
+    weights = (wq, wk)
+    x_groups = x.flatten_outer_dims().rearrange(
+        "(g p r) k -> g p (r k)", p=P, r=TILES_PER_GROUP
+    )
+    out_groups = [
+        out.rearrange("b t h d -> (b t) (h d)").rearrange(
+            "(g p r) c -> g p r c", p=P, r=TILES_PER_GROUP
+        )
+        for out in (out_0, out_1)
+    ]
+
+    with ExitStack() as stack:
+        consts = stack.enter_context(tc.tile_pool(name="consts", bufs=1))
+        raw = stack.enter_context(tc.tile_pool(name="raw", bufs=1))
+        x_pool = stack.enter_context(tc.tile_pool(name="x_pool", bufs=GROUPS))
+        grouped_pool = stack.enter_context(tc.tile_pool(name="grouped_pool", bufs=3))
+        quantised = stack.enter_context(tc.tile_pool(name="quantised", bufs=3))
+        terms = stack.enter_context(tc.tile_pool(name="terms", bufs=4))
+        results = stack.enter_context(tc.tile_pool(name="results", bufs=4))
+        flipped_pool = stack.enter_context(tc.psum_pool(name="flipped_pool", bufs=2))
+        product_pool = stack.enter_context(tc.psum_pool(name="product_pool", bufs=6))
+
+        w_raw = [raw.tile([P, 2 * 2 * CHANNELS], BF16, name="w_raw%d" % j) for j in range(2)]
+        x_raw = []
+
+        def load_weight(j):
+            nc.sync.dma_start(
+                out=w_raw[j][:].rearrange("p (h f) -> p h f", h=2),
+                in_=weights[j].rearrange("(h p e) k -> p h (e k)", h=2, p=P, e=2),
+            )
+
+        def load_group(g):
+            x_group = x_pool.tile([P, TILES_PER_GROUP * CHANNELS], BF16)
+            nc.sync.dma_start(out=x_group[:], in_=x_groups[g])
+            x_raw.append(x_group)
+
+        load_weight(0)
+        load_group(0)
+        load_weight(1)
+        for g in range(1, GROUPS):
+            load_group(g)
+
+        identity = consts.tile([P, P], F32)
+        make_identity(nc, identity[:])
+        cos, neg_cos, sin = build_cos_sin(nc, consts)
+
+        def quantise_weight(j):
+            odd_rows = w_raw[j][:].rearrange("p (h e k) -> p h e k", h=2, e=2)[:, :, 1, :]
+            nc.vector.tensor_scalar(
+                out=odd_rows, in0=odd_rows, scalar1=-1.0, scalar2=None, op0=ALU.mult
+            )
+            words = w_raw[j][:].bitcast(F32)
+            grouped = grouped_pool.tile([P, 4 * CHANNELS], BF16, align_bytes=64)
+            grouped_words = grouped[:].bitcast(F32).rearrange("p (c u) -> p c u", u=2)
+            for half, e in enumerate((1, 0)):
+                flipped = flipped_pool.tile([P, 2 * PAIRS], F32)
+                for u in range(2):
+                    for h in range(2):
+                        start = (2 * h + e) * WORDS + u * P
+                        nc.tensor.transpose(
+                            flipped[:, u * PAIRS + h * P : u * PAIRS + (h + 1) * P],
+                            words[:, start : start + P],
+                            identity[:],
+                        )
+                nc.vector.tensor_copy(
+                    out=grouped_words[:, half * PAIRS : (half + 1) * PAIRS, :],
+                    in_=flipped[:].rearrange("p (u c) -> p c u", u=2),
+                )
+            codes = consts.tile([P, CHANNELS], U32, name="w_codes%d" % j, align_bytes=64)
+            scales = consts.tile([P, CHANNELS], U8, name="w_scales%d" % j, align_bytes=64)
+            nc.vector.quantize_mx(out=codes[:].bitcast(FP8X4), scales=scales[:], in_=grouped[:])
+            return codes, scales
+
+        def quantise_group(g):
+            words = x_raw[g][:].bitcast(F32)
+            grouped = grouped_pool.tile([P, 4 * GROUP_TOKENS], BF16, align_bytes=64)
+            grouped_words = grouped[:].bitcast(F32).rearrange(
+                "p (r c u) -> p r c u", r=TILES_PER_GROUP, u=2
+            )
+            for first in range(0, TILES_PER_GROUP, TILES_PER_BANK):
+                flipped = flipped_pool.tile([P, TILES_PER_BANK * 2 * P], F32)
+                for r in range(TILES_PER_BANK):
+                    for u in range(2):
+                        start = (first + r) * WORDS + u * P
+                        nc.tensor.transpose(
+                            flipped[:, (2 * r + u) * P : (2 * r + u + 1) * P],
+                            words[:, start : start + P],
+                            identity[:],
+                        )
+                nc.scalar.copy(
+                    out=grouped_words[:, first : first + TILES_PER_BANK, :, :],
+                    in_=flipped[:].rearrange("p (r u c) -> p r c u", r=TILES_PER_BANK, u=2),
+                )
+            codes = quantised.tile([P, GROUP_TOKENS], U32, align_bytes=64)
+            scales = quantised.tile([P, GROUP_TOKENS], U8, align_bytes=64)
+            nc.vector.quantize_mx(out=codes[:].bitcast(FP8X4), scales=scales[:], in_=grouped[:])
+            return codes, scales
+
+        def project_and_rotate(g, x_codes, x_scales):
+            for first in range(0, TILES_PER_GROUP, TILES_PER_STORE):
+                rotated = [
+                    results.tile([P, TILES_PER_STORE, CHANNELS], F32, name="rotated%d" % j)
+                    for j in range(2)
+                ]
+                for r in range(TILES_PER_STORE):
+                    token_tile = slice((first + r) * P, (first + r + 1) * P)
+                    column = (g % GROUPS_PER_SEQ) * TILES_PER_GROUP + first + r
+                    for j in range(2):
+                        product = product_pool.tile([P, CHANNELS], F32)
+                        nc.tensor.matmul_mx(
+                            out=product[:],
+                            lhsT=x_codes[:, token_tile].bitcast(FP8X4),
+                            lhsT_scale=x_scales[:, token_tile],
+                            rhs=w_codes[j][:].bitcast(FP8X4),
+                            rhs_scale=w_scales[j][:],
+                            start=True,
+                            stop=True,
+                        )
+                        second = terms.tile([P, 2, PAIRS], F32)
+                        nc.scalar.activation(
+                            out=second[:, 0, :], in_=product[:, PAIRS:], func=ACT.Copy,
+                            scale=cos[:, column : column + 1],
+                        )
+                        nc.scalar.activation(
+                            out=second[:, 1, :], in_=product[:, :PAIRS], func=ACT.Copy,
+                            scale=neg_cos[:, column : column + 1],
+                        )
+                        nc.vector.scalar_tensor_tensor(
+                            out=rotated[j][:, r, :].rearrange("p (i e) -> p i e", e=2),
+                            in0=product[:].rearrange("p (e i) -> p i e", e=2),
+                            scalar=sin[:, column : column + 1],
+                            in1=second[:].rearrange("p e i -> p i e"),
+                            op0=ALU.mult,
+                            op1=ALU.add,
+                        )
+                for j in range(2):
+                    nc.sync.dma_start(
+                        out=out_groups[j][g][:, first : first + TILES_PER_STORE, :],
+                        in_=rotated[j][:],
+                    )
+
+        w_codes = [None, None]
+        w_scales = [None, None]
+        w_codes[0], w_scales[0] = quantise_weight(0)
+        ready = quantise_group(0)
+        w_codes[1], w_scales[1] = quantise_weight(1)
+        for g in range(GROUPS):
+            current = ready
+            if g + 1 < GROUPS:
+                ready = quantise_group(g + 1)
+            project_and_rotate(g, current[0], current[1])

@@ -21,8 +21,11 @@ TILES_PER_GROUP = 4
 GROUP_TOKENS = P * TILES_PER_GROUP
 GROUPS = TOKENS // GROUP_TOKENS
 GROUPS_PER_SEQ = SEQ // GROUP_TOKENS
-TILES_PER_BANK = 2
+ANGLES = GROUPS_PER_SEQ * TILES_PER_GROUP
 TILES_PER_STORE = 2
+PSUM_BANKS = 8
+BANK = 512
+REGROUP_AT = 2
 
 FLOPS = 2 * TOKENS * CHANNELS * 2 * CHANNELS
 
@@ -31,9 +34,8 @@ TWO_PI_HIGH = round(2.0 * math.pi * 2.0**13) / 2.0**13
 TWO_PI_LOW = 2.0 * math.pi - TWO_PI_HIGH
 
 
-def build_cos_sin(nc, consts):
-    columns = GROUPS_PER_SEQ * TILES_PER_GROUP
-    position = consts.tile([P, columns], F32)
+def half_angle_sines(nc, consts):
+    position = consts.tile([P, ANGLES], F32)
     nc.gpsimd.iota(
         position[:],
         pattern=[[GROUP_TOKENS, GROUPS_PER_SEQ], [1, TILES_PER_GROUP]],
@@ -41,49 +43,53 @@ def build_cos_sin(nc, consts):
         channel_multiplier=TILES_PER_GROUP,
         allow_small_or_imprecise_dtypes=True,
     )
-    shifted = consts.tile([P, columns], F32)
+    shifted = consts.tile([P, ANGLES], F32)
     nc.vector.tensor_scalar(
         out=shifted[:], in0=position[:], scalar1=1.0 / (2.0 * math.pi), scalar2=ROUND_TO_WHOLE,
         op0=ALU.mult, op1=ALU.add,
     )
-    turns = consts.tile([P, columns], F32)
+    turns = consts.tile([P, ANGLES], F32)
     nc.vector.tensor_scalar(
         out=turns[:], in0=shifted[:], scalar1=ROUND_TO_WHOLE, scalar2=None, op0=ALU.subtract
     )
-    coarse = consts.tile([P, columns], F32)
+    coarse = consts.tile([P, ANGLES], F32)
     nc.vector.scalar_tensor_tensor(
         out=coarse[:], in0=turns[:], scalar=-TWO_PI_HIGH, in1=position[:], op0=ALU.mult, op1=ALU.add
     )
-    angle = consts.tile([P, columns], F32)
+    angle = consts.tile([P, ANGLES], F32)
     nc.vector.scalar_tensor_tensor(
         out=angle[:], in0=turns[:], scalar=-TWO_PI_LOW, in1=coarse[:], op0=ALU.mult, op1=ALU.add
     )
-    magnitude = consts.tile([P, columns], F32)
+    magnitude = consts.tile([P, ANGLES], F32)
     nc.vector.scalar_tensor_tensor(
         out=magnitude[:], in0=angle[:], scalar=-1.0, in1=angle[:], op0=ALU.mult, op1=ALU.max
     )
-    sin_half = consts.tile([P, columns], F32)
-    nc.scalar.activation(out=sin_half[:], in_=angle[:], func=ACT.Sin, scale=0.5)
-    complement = consts.tile([P, columns], F32)
+    complement = consts.tile([P, ANGLES], F32)
     nc.vector.tensor_scalar(
         out=complement[:], in0=magnitude[:], scalar1=-0.5, scalar2=math.pi / 2.0,
         op0=ALU.mult, op1=ALU.add,
     )
-    cos_half = consts.tile([P, columns], F32)
+    sin_half = consts.tile([P, ANGLES], F32)
+    nc.scalar.activation(out=sin_half[:], in_=angle[:], func=ACT.Sin, scale=0.5)
+    cos_half = consts.tile([P, ANGLES], F32)
     nc.scalar.activation(out=cos_half[:], in_=complement[:], func=ACT.Sin)
-    sin = consts.tile([P, columns], F32)
+    return sin_half, cos_half
+
+
+def double_angles(nc, consts, sin_half, cos_half):
+    sin = consts.tile([P, ANGLES], F32)
     nc.vector.scalar_tensor_tensor(
         out=sin[:], in0=sin_half[:], scalar=2.0, in1=cos_half[:], op0=ALU.mult, op1=ALU.mult
     )
-    cos_less_one = consts.tile([P, columns], F32)
+    cos_less_one = consts.tile([P, ANGLES], F32)
     nc.vector.scalar_tensor_tensor(
         out=cos_less_one[:], in0=sin_half[:], scalar=-2.0, in1=sin_half[:], op0=ALU.mult, op1=ALU.mult
     )
-    cos = consts.tile([P, columns], F32)
+    cos = consts.tile([P, ANGLES], F32)
     nc.vector.tensor_scalar(
         out=cos[:], in0=cos_less_one[:], scalar1=1.0, scalar2=None, op0=ALU.add
     )
-    neg_cos = consts.tile([P, columns], F32)
+    neg_cos = consts.tile([P, ANGLES], F32)
     nc.vector.tensor_scalar(
         out=neg_cos[:], in0=cos_less_one[:], scalar1=-1.0, scalar2=-1.0, op0=ALU.mult, op1=ALU.add
     )
@@ -105,17 +111,16 @@ def tile_attention_pa_t_kernel(tc, x, wq, wk, out_0, out_1):
 
     with ExitStack() as stack:
         consts = stack.enter_context(tc.tile_pool(name="consts", bufs=1))
-        raw = stack.enter_context(tc.tile_pool(name="raw", bufs=1))
         x_pool = stack.enter_context(tc.tile_pool(name="x_pool", bufs=GROUPS))
         grouped_pool = stack.enter_context(tc.tile_pool(name="grouped_pool", bufs=3))
         quantised = stack.enter_context(tc.tile_pool(name="quantised", bufs=3))
         terms = stack.enter_context(tc.tile_pool(name="terms", bufs=4))
         results = stack.enter_context(tc.tile_pool(name="results", bufs=4))
-        flipped_pool = stack.enter_context(tc.psum_pool(name="flipped_pool", bufs=2))
-        product_pool = stack.enter_context(tc.psum_pool(name="product_pool", bufs=6))
+        banks = stack.enter_context(tc.psum_pool(name="banks", bufs=PSUM_BANKS))
+        stack.enter_context(tc.manual_schedule())
 
-        w_raw = [raw.tile([P, 2 * 2 * CHANNELS], BF16, name="w_raw%d" % j) for j in range(2)]
-        x_raw = []
+        w_raw = [consts.tile([P, 2 * 2 * CHANNELS], BF16, name="w_raw%d" % j) for j in range(2)]
+        x_raw = [x_pool.tile([P, TILES_PER_GROUP * CHANNELS], BF16, name="x_raw") for g in range(GROUPS)]
 
         def load_weight(j):
             nc.sync.dma_start(
@@ -123,123 +128,119 @@ def tile_attention_pa_t_kernel(tc, x, wq, wk, out_0, out_1):
                 in_=weights[j].rearrange("(h p e) k -> p h (e k)", h=2, p=P, e=2),
             )
 
-        def load_group(g):
-            x_group = x_pool.tile([P, TILES_PER_GROUP * CHANNELS], BF16)
-            nc.sync.dma_start(out=x_group[:], in_=x_groups[g])
-            x_raw.append(x_group)
-
         load_weight(0)
-        load_group(0)
+        nc.sync.dma_start(out=x_raw[0][:], in_=x_groups[0])
         load_weight(1)
         for g in range(1, GROUPS):
-            load_group(g)
+            nc.sync.dma_start(out=x_raw[g][:], in_=x_groups[g])
 
+        sin_half, cos_half = half_angle_sines(nc, consts)
         identity = consts.tile([P, P], F32)
         make_identity(nc, identity[:])
-        cos, neg_cos, sin = build_cos_sin(nc, consts)
 
-        def quantise_weight(j):
+        def negate_odd_rows(j):
             odd_rows = w_raw[j][:].rearrange("p (h e k) -> p h e k", h=2, e=2)[:, :, 1, :]
             nc.vector.tensor_scalar(
                 out=odd_rows, in0=odd_rows, scalar1=-1.0, scalar2=None, op0=ALU.mult
             )
+
+        def transpose_words(words, starts):
+            flipped = banks.tile([P, BANK], F32, tag="bank")
+            for n, start in enumerate(starts):
+                nc.tensor.transpose(
+                    flipped[:, n * P : (n + 1) * P], words[:, start : start + P], identity[:]
+                )
+            return flipped
+
+        def regroup_weight(j):
             words = w_raw[j][:].bitcast(F32)
             grouped = grouped_pool.tile([P, 4 * CHANNELS], BF16, align_bytes=64)
-            grouped_words = grouped[:].bitcast(F32).rearrange("p (c u) -> p c u", u=2)
-            for half, e in enumerate((1, 0)):
-                flipped = flipped_pool.tile([P, 2 * PAIRS], F32)
-                for u in range(2):
-                    for h in range(2):
-                        start = (2 * h + e) * WORDS + u * P
-                        nc.tensor.transpose(
-                            flipped[:, u * PAIRS + h * P : u * PAIRS + (h + 1) * P],
-                            words[:, start : start + P],
-                            identity[:],
-                        )
-                nc.vector.tensor_copy(
-                    out=grouped_words[:, half * PAIRS : (half + 1) * PAIRS, :],
-                    in_=flipped[:].rearrange("p (u c) -> p c u", u=2),
-                )
-            codes = consts.tile([P, CHANNELS], U32, name="w_codes%d" % j, align_bytes=64)
-            scales = consts.tile([P, CHANNELS], U8, name="w_scales%d" % j, align_bytes=64)
-            nc.vector.quantize_mx(out=codes[:].bitcast(FP8X4), scales=scales[:], in_=grouped[:])
-            return codes, scales
+            halves = grouped[:].bitcast(F32).rearrange("p (n c u) -> p n c u", n=2, u=2)
+            even = transpose_words(words, [(2 * h + 0) * WORDS + u * P for u in range(2) for h in range(2)])
+            nc.scalar.copy(out=halves[:, 1, :, :], in_=even[:].rearrange("p (u c) -> p c u", u=2))
+            odd = transpose_words(words, [(2 * h + 1) * WORDS + u * P for u in range(2) for h in range(2)])
+            nc.vector.tensor_copy(out=halves[:, 0, :, :], in_=odd[:].rearrange("p (u c) -> p c u", u=2))
+            return grouped
 
-        def quantise_group(g):
+        def regroup_tokens(g):
             words = x_raw[g][:].bitcast(F32)
             grouped = grouped_pool.tile([P, 4 * GROUP_TOKENS], BF16, align_bytes=64)
-            grouped_words = grouped[:].bitcast(F32).rearrange(
-                "p (r c u) -> p r c u", r=TILES_PER_GROUP, u=2
+            halves = grouped[:].bitcast(F32).rearrange("p (n r c u) -> p n r c u", n=2, r=2, u=2)
+            first = transpose_words(words, [r * WORDS + u * P for r in (0, 1) for u in range(2)])
+            nc.scalar.copy(
+                out=halves[:, 0, :, :, :], in_=first[:].rearrange("p (r u c) -> p r c u", r=2, u=2)
             )
-            for first in range(0, TILES_PER_GROUP, TILES_PER_BANK):
-                flipped = flipped_pool.tile([P, TILES_PER_BANK * 2 * P], F32)
-                for r in range(TILES_PER_BANK):
-                    for u in range(2):
-                        start = (first + r) * WORDS + u * P
-                        nc.tensor.transpose(
-                            flipped[:, (2 * r + u) * P : (2 * r + u + 1) * P],
-                            words[:, start : start + P],
-                            identity[:],
-                        )
-                nc.scalar.copy(
-                    out=grouped_words[:, first : first + TILES_PER_BANK, :, :],
-                    in_=flipped[:].rearrange("p (r u c) -> p r c u", r=TILES_PER_BANK, u=2),
-                )
-            codes = quantised.tile([P, GROUP_TOKENS], U32, align_bytes=64)
-            scales = quantised.tile([P, GROUP_TOKENS], U8, align_bytes=64)
+            last = transpose_words(words, [r * WORDS + u * P for r in (2, 3) for u in range(2)])
+            nc.vector.tensor_copy(
+                out=halves[:, 1, :, :, :], in_=last[:].rearrange("p (r u c) -> p r c u", r=2, u=2)
+            )
+            return grouped
+
+        def quantise(pool, name, grouped):
+            codes = pool.tile([P, BANK], U32, name=name + "_codes", align_bytes=64)
+            scales = pool.tile([P, BANK], U8, name=name + "_scales", align_bytes=64)
             nc.vector.quantize_mx(out=codes[:].bitcast(FP8X4), scales=scales[:], in_=grouped[:])
             return codes, scales
 
-        def project_and_rotate(g, x_codes, x_scales):
-            for first in range(0, TILES_PER_GROUP, TILES_PER_STORE):
-                rotated = [
-                    results.tile([P, TILES_PER_STORE, CHANNELS], F32, name="rotated%d" % j)
-                    for j in range(2)
-                ]
-                for r in range(TILES_PER_STORE):
-                    token_tile = slice((first + r) * P, (first + r + 1) * P)
-                    column = (g % GROUPS_PER_SEQ) * TILES_PER_GROUP + first + r
-                    for j in range(2):
-                        product = product_pool.tile([P, CHANNELS], F32)
-                        nc.tensor.matmul_mx(
-                            out=product[:],
-                            lhsT=x_codes[:, token_tile].bitcast(FP8X4),
-                            lhsT_scale=x_scales[:, token_tile],
-                            rhs=w_codes[j][:].bitcast(FP8X4),
-                            rhs_scale=w_scales[j][:],
-                            start=True,
-                            stop=True,
-                        )
-                        second = terms.tile([P, 2, PAIRS], F32)
-                        nc.scalar.activation(
-                            out=second[:, 0, :], in_=product[:, PAIRS:], func=ACT.Copy,
-                            scale=cos[:, column : column + 1],
-                        )
-                        nc.scalar.activation(
-                            out=second[:, 1, :], in_=product[:, :PAIRS], func=ACT.Copy,
-                            scale=neg_cos[:, column : column + 1],
-                        )
-                        nc.vector.scalar_tensor_tensor(
-                            out=rotated[j][:, r, :].rearrange("p (i e) -> p i e", e=2),
-                            in0=product[:].rearrange("p (e i) -> p i e", e=2),
-                            scalar=sin[:, column : column + 1],
-                            in1=second[:].rearrange("p e i -> p i e"),
-                            op0=ALU.mult,
-                            op1=ALU.add,
-                        )
-                for j in range(2):
-                    nc.sync.dma_start(
-                        out=out_groups[j][g][:, first : first + TILES_PER_STORE, :],
-                        in_=rotated[j][:],
-                    )
+        def project_and_rotate(x_mx, w_mx, r, column, rotated):
+            token_tile = slice(r * P, (r + 1) * P)
+            product = banks.tile([P, BANK], F32, tag="bank")
+            nc.tensor.matmul_mx(
+                out=product[:],
+                lhsT=x_mx[0][:, token_tile].bitcast(FP8X4),
+                lhsT_scale=x_mx[1][:, token_tile],
+                rhs=w_mx[0][:].bitcast(FP8X4),
+                rhs_scale=w_mx[1][:],
+                start=True,
+                stop=True,
+            )
+            second = terms.tile([P, 2, PAIRS], F32)
+            nc.scalar.activation(
+                out=second[:, 0, :], in_=product[:, PAIRS:], func=ACT.Copy,
+                scale=cos[:, column : column + 1],
+            )
+            nc.scalar.activation(
+                out=second[:, 1, :], in_=product[:, :PAIRS], func=ACT.Copy,
+                scale=neg_cos[:, column : column + 1],
+            )
+            nc.vector.scalar_tensor_tensor(
+                out=rotated.rearrange("p (i e) -> p i e", e=2),
+                in0=product[:].rearrange("p (e i) -> p i e", e=2),
+                scalar=sin[:, column : column + 1],
+                in1=second[:].rearrange("p e i -> p i e"),
+                op0=ALU.mult,
+                op1=ALU.add,
+            )
 
-        w_codes = [None, None]
-        w_scales = [None, None]
-        w_codes[0], w_scales[0] = quantise_weight(0)
-        ready = quantise_group(0)
-        w_codes[1], w_scales[1] = quantise_weight(1)
+        negate_odd_rows(0)
+        grouped_wq = regroup_weight(0)
+        wq_mx = quantise(consts, "wq", grouped_wq)
+        negate_odd_rows(1)
+        grouped_x = regroup_tokens(0)
+        cos, neg_cos, sin = double_angles(nc, consts, sin_half, cos_half)
+        next_x_mx = quantise(quantised, "x", grouped_x)
+        grouped_wk = regroup_weight(1)
+        wk_mx = quantise(consts, "wk", grouped_wk)
+        w_mx = (wq_mx, wk_mx)
+
         for g in range(GROUPS):
-            current = ready
-            if g + 1 < GROUPS:
-                ready = quantise_group(g + 1)
-            project_and_rotate(g, current[0], current[1])
+            x_mx = next_x_mx
+            for r in range(TILES_PER_GROUP):
+                if r % TILES_PER_STORE == 0:
+                    rotated = [
+                        results.tile([P, TILES_PER_STORE, CHANNELS], F32, name="rotated%d" % j)
+                        for j in range(2)
+                    ]
+                column = (g % GROUPS_PER_SEQ) * TILES_PER_GROUP + r
+                for j in range(2):
+                    if g + 1 < GROUPS and 2 * r + j == REGROUP_AT:
+                        grouped_x = regroup_tokens(g + 1)
+                    if g + 1 < GROUPS and 2 * r + j == REGROUP_AT + 1:
+                        next_x_mx = quantise(quantised, "x", grouped_x)
+                    project_and_rotate(x_mx, w_mx[j], r, column, rotated[j][:, r % TILES_PER_STORE, :])
+                    if r % TILES_PER_STORE == TILES_PER_STORE - 1:
+                        first_tile = r + 1 - TILES_PER_STORE
+                        nc.sync.dma_start(
+                            out=out_groups[j][g][:, first_tile : first_tile + TILES_PER_STORE, :],
+                            in_=rotated[j][:],
+                        )

@@ -26,6 +26,7 @@ TILES_PER_STORE = 2
 PSUM_BANKS = 8
 BANK = 512
 REGROUP_AT = 2
+GPSIMD_AT = 0
 
 FLOPS = 2 * TOKENS * CHANNELS * 2 * CHANNELS
 
@@ -115,6 +116,7 @@ def tile_attention_pa_t_kernel(tc, x, wq, wk, out_0, out_1):
         grouped_pool = stack.enter_context(tc.tile_pool(name="grouped_pool", bufs=3))
         quantised = stack.enter_context(tc.tile_pool(name="quantised", bufs=3))
         terms = stack.enter_context(tc.tile_pool(name="terms", bufs=4))
+        gpsimd_terms = stack.enter_context(tc.tile_pool(name="gpsimd_terms", bufs=2))
         results = stack.enter_context(tc.tile_pool(name="results", bufs=4))
         banks = stack.enter_context(tc.psum_pool(name="banks", bufs=PSUM_BANKS))
         stack.enter_context(tc.manual_schedule())
@@ -182,7 +184,7 @@ def tile_attention_pa_t_kernel(tc, x, wq, wk, out_0, out_1):
             nc.vector.quantize_mx(out=codes[:].bitcast(FP8X4), scales=scales[:], in_=grouped[:])
             return codes, scales
 
-        def project_and_rotate(x_mx, w_mx, r, column, rotated):
+        def project(x_mx, w_mx, r):
             token_tile = slice(r * P, (r + 1) * P)
             product = banks.tile([P, BANK], F32, tag="bank")
             nc.tensor.matmul_mx(
@@ -194,6 +196,9 @@ def tile_attention_pa_t_kernel(tc, x, wq, wk, out_0, out_1):
                 start=True,
                 stop=True,
             )
+            return product
+
+        def rotate(product, column, rotated):
             second = terms.tile([P, 2, PAIRS], F32)
             nc.scalar.activation(
                 out=second[:, 0, :], in_=product[:, PAIRS:], func=ACT.Copy,
@@ -210,6 +215,30 @@ def tile_attention_pa_t_kernel(tc, x, wq, wk, out_0, out_1):
                 in1=second[:].rearrange("p e i -> p i e"),
                 op0=ALU.mult,
                 op1=ALU.add,
+            )
+
+        def rotate_on_gpsimd(product, column, rotated):
+            copied = gpsimd_terms.tile([P, 2, PAIRS], F32)
+            nc.scalar.copy(out=copied[:].rearrange("p e i -> p (e i)"), in_=product[:])
+            second = gpsimd_terms.tile([P, 2, PAIRS], F32, name="gpsimd_second")
+            nc.gpsimd.tensor_scalar(
+                out=second[:, 0, :], in0=copied[:, 1, :], scalar1=cos[:, column : column + 1],
+                scalar2=0.0, op0=ALU.mult, op1=ALU.add,
+            )
+            nc.gpsimd.tensor_scalar(
+                out=second[:, 1, :], in0=copied[:, 0, :], scalar1=neg_cos[:, column : column + 1],
+                scalar2=0.0, op0=ALU.mult, op1=ALU.add,
+            )
+            first = gpsimd_terms.tile([P, 2, PAIRS], F32, name="gpsimd_first")
+            nc.gpsimd.tensor_scalar(
+                out=first[:], in0=copied[:], scalar1=sin[:, column : column + 1],
+                scalar2=0.0, op0=ALU.mult, op1=ALU.add,
+            )
+            nc.gpsimd.tensor_tensor(
+                out=rotated.rearrange("p (i e) -> p i e", e=2),
+                in0=first[:].rearrange("p e i -> p i e"),
+                in1=second[:].rearrange("p e i -> p i e"),
+                op=ALU.add,
             )
 
         negate_odd_rows(0)
@@ -237,7 +266,11 @@ def tile_attention_pa_t_kernel(tc, x, wq, wk, out_0, out_1):
                         grouped_x = regroup_tokens(g + 1)
                     if g + 1 < GROUPS and 2 * r + j == REGROUP_AT + 1:
                         next_x_mx = quantise(quantised, "x", grouped_x)
-                    project_and_rotate(x_mx, w_mx[j], r, column, rotated[j][:, r % TILES_PER_STORE, :])
+                    product = project(x_mx, w_mx[j], r)
+                    if 2 * r + j == GPSIMD_AT:
+                        rotate_on_gpsimd(product, column, rotated[j][:, r % TILES_PER_STORE, :])
+                    else:
+                        rotate(product, column, rotated[j][:, r % TILES_PER_STORE, :])
                     if r % TILES_PER_STORE == TILES_PER_STORE - 1:
                         first_tile = r + 1 - TILES_PER_STORE
                         nc.sync.dma_start(

@@ -26,7 +26,6 @@ TILES_PER_STORE = 2
 PSUM_BANKS = 8
 BANK = 512
 REGROUP_AT = 2
-GPSIMD_AT = 0
 
 FLOPS = 2 * TOKENS * CHANNELS * 2 * CHANNELS
 
@@ -116,8 +115,7 @@ def tile_attention_pa_t_kernel(tc, x, wq, wk, out_0, out_1):
         grouped_pool = stack.enter_context(tc.tile_pool(name="grouped_pool", bufs=3))
         quantised = stack.enter_context(tc.tile_pool(name="quantised", bufs=3))
         terms = stack.enter_context(tc.tile_pool(name="terms", bufs=4))
-        gpsimd_terms = stack.enter_context(tc.tile_pool(name="gpsimd_terms", bufs=2))
-        results = stack.enter_context(tc.tile_pool(name="results", bufs=4))
+        results = stack.enter_context(tc.tile_pool(name="results", bufs=8))
         banks = stack.enter_context(tc.psum_pool(name="banks", bufs=PSUM_BANKS))
         stack.enter_context(tc.manual_schedule())
 
@@ -154,17 +152,25 @@ def tile_attention_pa_t_kernel(tc, x, wq, wk, out_0, out_1):
                 )
             return flipped
 
-        def regroup_weight(j):
+        def copy_second_bank(vector_helps, out, in_):
+            if vector_helps:
+                nc.vector.tensor_copy(out=out, in_=in_)
+            else:
+                nc.scalar.copy(out=out, in_=in_)
+
+        def regroup_weight(j, vector_helps):
             words = w_raw[j][:].bitcast(F32)
             grouped = grouped_pool.tile([P, 4 * CHANNELS], BF16, align_bytes=64)
             halves = grouped[:].bitcast(F32).rearrange("p (n c u) -> p n c u", n=2, u=2)
             even = transpose_words(words, [(2 * h + 0) * WORDS + u * P for u in range(2) for h in range(2)])
             nc.scalar.copy(out=halves[:, 1, :, :], in_=even[:].rearrange("p (u c) -> p c u", u=2))
             odd = transpose_words(words, [(2 * h + 1) * WORDS + u * P for u in range(2) for h in range(2)])
-            nc.vector.tensor_copy(out=halves[:, 0, :, :], in_=odd[:].rearrange("p (u c) -> p c u", u=2))
+            copy_second_bank(
+                vector_helps, halves[:, 0, :, :], odd[:].rearrange("p (u c) -> p c u", u=2)
+            )
             return grouped
 
-        def regroup_tokens(g):
+        def regroup_tokens(g, vector_helps):
             words = x_raw[g][:].bitcast(F32)
             grouped = grouped_pool.tile([P, 4 * GROUP_TOKENS], BF16, align_bytes=64)
             halves = grouped[:].bitcast(F32).rearrange("p (n r c u) -> p n r c u", n=2, r=2, u=2)
@@ -173,8 +179,8 @@ def tile_attention_pa_t_kernel(tc, x, wq, wk, out_0, out_1):
                 out=halves[:, 0, :, :, :], in_=first[:].rearrange("p (r u c) -> p r c u", r=2, u=2)
             )
             last = transpose_words(words, [r * WORDS + u * P for r in (2, 3) for u in range(2)])
-            nc.vector.tensor_copy(
-                out=halves[:, 1, :, :, :], in_=last[:].rearrange("p (r u c) -> p r c u", r=2, u=2)
+            copy_second_bank(
+                vector_helps, halves[:, 1, :, :, :], last[:].rearrange("p (r u c) -> p r c u", r=2, u=2)
             )
             return grouped
 
@@ -184,7 +190,7 @@ def tile_attention_pa_t_kernel(tc, x, wq, wk, out_0, out_1):
             nc.vector.quantize_mx(out=codes[:].bitcast(FP8X4), scales=scales[:], in_=grouped[:])
             return codes, scales
 
-        def project(x_mx, w_mx, r):
+        def project_and_rotate(x_mx, w_mx, r, column, rotated):
             token_tile = slice(r * P, (r + 1) * P)
             product = banks.tile([P, BANK], F32, tag="bank")
             nc.tensor.matmul_mx(
@@ -196,9 +202,6 @@ def tile_attention_pa_t_kernel(tc, x, wq, wk, out_0, out_1):
                 start=True,
                 stop=True,
             )
-            return product
-
-        def rotate(product, column, rotated):
             second = terms.tile([P, 2, PAIRS], F32)
             nc.scalar.activation(
                 out=second[:, 0, :], in_=product[:, PAIRS:], func=ACT.Copy,
@@ -217,63 +220,37 @@ def tile_attention_pa_t_kernel(tc, x, wq, wk, out_0, out_1):
                 op1=ALU.add,
             )
 
-        def rotate_on_gpsimd(product, column, rotated):
-            copied = gpsimd_terms.tile([P, 2, PAIRS], F32)
-            nc.scalar.copy(out=copied[:].rearrange("p e i -> p (e i)"), in_=product[:])
-            second = gpsimd_terms.tile([P, 2, PAIRS], F32, name="gpsimd_second")
-            nc.gpsimd.tensor_scalar(
-                out=second[:, 0, :], in0=copied[:, 1, :], scalar1=cos[:, column : column + 1],
-                scalar2=0.0, op0=ALU.mult, op1=ALU.add,
-            )
-            nc.gpsimd.tensor_scalar(
-                out=second[:, 1, :], in0=copied[:, 0, :], scalar1=neg_cos[:, column : column + 1],
-                scalar2=0.0, op0=ALU.mult, op1=ALU.add,
-            )
-            first = gpsimd_terms.tile([P, 2, PAIRS], F32, name="gpsimd_first")
-            nc.gpsimd.tensor_scalar(
-                out=first[:], in0=copied[:], scalar1=sin[:, column : column + 1],
-                scalar2=0.0, op0=ALU.mult, op1=ALU.add,
-            )
-            nc.gpsimd.tensor_tensor(
-                out=rotated.rearrange("p (i e) -> p i e", e=2),
-                in0=first[:].rearrange("p e i -> p i e"),
-                in1=second[:].rearrange("p e i -> p i e"),
-                op=ALU.add,
-            )
-
+        cos, neg_cos, sin = double_angles(nc, consts, sin_half, cos_half)
         negate_odd_rows(0)
-        grouped_wq = regroup_weight(0)
+        grouped_wq = regroup_weight(0, vector_helps=True)
         wq_mx = quantise(consts, "wq", grouped_wq)
         negate_odd_rows(1)
-        grouped_x = regroup_tokens(0)
-        cos, neg_cos, sin = double_angles(nc, consts, sin_half, cos_half)
+        grouped_x = regroup_tokens(0, vector_helps=False)
         next_x_mx = quantise(quantised, "x", grouped_x)
-        grouped_wk = regroup_weight(1)
+        grouped_wk = regroup_weight(1, vector_helps=False)
         wk_mx = quantise(consts, "wk", grouped_wk)
         w_mx = (wq_mx, wk_mx)
 
         for g in range(GROUPS):
             x_mx = next_x_mx
-            for r in range(TILES_PER_GROUP):
-                if r % TILES_PER_STORE == 0:
-                    rotated = [
-                        results.tile([P, TILES_PER_STORE, CHANNELS], F32, name="rotated%d" % j)
-                        for j in range(2)
-                    ]
-                column = (g % GROUPS_PER_SEQ) * TILES_PER_GROUP + r
+            last_group = g == GROUPS - 1
+            made = 0
+            for first_tile in range(0, TILES_PER_GROUP, TILES_PER_STORE):
                 for j in range(2):
-                    if g + 1 < GROUPS and 2 * r + j == REGROUP_AT:
-                        grouped_x = regroup_tokens(g + 1)
-                    if g + 1 < GROUPS and 2 * r + j == REGROUP_AT + 1:
-                        next_x_mx = quantise(quantised, "x", grouped_x)
-                    product = project(x_mx, w_mx[j], r)
-                    if 2 * r + j == GPSIMD_AT:
-                        rotate_on_gpsimd(product, column, rotated[j][:, r % TILES_PER_STORE, :])
-                    else:
-                        rotate(product, column, rotated[j][:, r % TILES_PER_STORE, :])
-                    if r % TILES_PER_STORE == TILES_PER_STORE - 1:
-                        first_tile = r + 1 - TILES_PER_STORE
+                    rotated = results.tile([P, TILES_PER_STORE, CHANNELS], F32)
+                    for n in range(TILES_PER_STORE):
+                        r = first_tile + n
+                        if not last_group and made == REGROUP_AT:
+                            grouped_x = regroup_tokens(g + 1, vector_helps=True)
+                        if not last_group and made == REGROUP_AT + 1:
+                            next_x_mx = quantise(quantised, "x", grouped_x)
+                        column = (g % GROUPS_PER_SEQ) * TILES_PER_GROUP + r
+                        project_and_rotate(x_mx, w_mx[j], r, column, rotated[:, n, :])
+                        made += 1
+                        if last_group:
+                            nc.sync.dma_start(out=out_groups[j][g][:, r, :], in_=rotated[:, n, :])
+                    if not last_group:
                         nc.sync.dma_start(
                             out=out_groups[j][g][:, first_tile : first_tile + TILES_PER_STORE, :],
-                            in_=rotated[j][:],
+                            in_=rotated[:],
                         )

import math
from contextlib import ExitStack

import concourse.mybir as mybir
from concourse.masks import make_identity

F32 = mybir.dt.float32
BF16 = mybir.dt.bfloat16
U32 = mybir.dt.uint32
U8 = mybir.dt.uint8
FP8X4 = mybir.dt.float8_e4m3fn_x4
ALU = mybir.AluOpType
ACT = mybir.ActivationFunctionType

P = 128
BATCH, SEQ, CHANNELS = 4, 1024, 512
TOKENS = BATCH * SEQ
PAIRS = CHANNELS // 2
WORDS = CHANNELS // 2
TILES_PER_GROUP = 4
GROUP_TOKENS = P * TILES_PER_GROUP
GROUPS = TOKENS // GROUP_TOKENS
GROUPS_PER_SEQ = SEQ // GROUP_TOKENS
ANGLES = GROUPS_PER_SEQ * TILES_PER_GROUP
TILES_PER_STORE = 2
PSUM_BANKS = 8
BANK = 512
REGROUP_AT = 2

FLOPS = 2 * TOKENS * CHANNELS * 2 * CHANNELS

ROUND_TO_WHOLE = 1.5 * 2.0**23
TWO_PI_HIGH = round(2.0 * math.pi * 2.0**13) / 2.0**13
TWO_PI_LOW = 2.0 * math.pi - TWO_PI_HIGH


def half_angle_sines(nc, consts):
    position = consts.tile([P, ANGLES], F32)
    nc.gpsimd.iota(
        position[:],
        pattern=[[GROUP_TOKENS, GROUPS_PER_SEQ], [1, TILES_PER_GROUP]],
        base=0,
        channel_multiplier=TILES_PER_GROUP,
        allow_small_or_imprecise_dtypes=True,
    )
    shifted = consts.tile([P, ANGLES], F32)
    nc.vector.tensor_scalar(
        out=shifted[:], in0=position[:], scalar1=1.0 / (2.0 * math.pi), scalar2=ROUND_TO_WHOLE,
        op0=ALU.mult, op1=ALU.add,
    )
    turns = consts.tile([P, ANGLES], F32)
    nc.vector.tensor_scalar(
        out=turns[:], in0=shifted[:], scalar1=ROUND_TO_WHOLE, scalar2=None, op0=ALU.subtract
    )
    coarse = consts.tile([P, ANGLES], F32)
    nc.vector.scalar_tensor_tensor(
        out=coarse[:], in0=turns[:], scalar=-TWO_PI_HIGH, in1=position[:], op0=ALU.mult, op1=ALU.add
    )
    angle = consts.tile([P, ANGLES], F32)
    nc.vector.scalar_tensor_tensor(
        out=angle[:], in0=turns[:], scalar=-TWO_PI_LOW, in1=coarse[:], op0=ALU.mult, op1=ALU.add
    )
    magnitude = consts.tile([P, ANGLES], F32)
    nc.vector.scalar_tensor_tensor(
        out=magnitude[:], in0=angle[:], scalar=-1.0, in1=angle[:], op0=ALU.mult, op1=ALU.max
    )
    complement = consts.tile([P, ANGLES], F32)
    nc.vector.tensor_scalar(
        out=complement[:], in0=magnitude[:], scalar1=-0.5, scalar2=math.pi / 2.0,
        op0=ALU.mult, op1=ALU.add,
    )
    sin_half = consts.tile([P, ANGLES], F32)
    nc.scalar.activation(out=sin_half[:], in_=angle[:], func=ACT.Sin, scale=0.5)
    cos_half = consts.tile([P, ANGLES], F32)
    nc.scalar.activation(out=cos_half[:], in_=complement[:], func=ACT.Sin)
    return sin_half, cos_half


def double_angles(nc, consts, sin_half, cos_half):
    sin = consts.tile([P, ANGLES], F32)
    nc.vector.scalar_tensor_tensor(
        out=sin[:], in0=sin_half[:], scalar=2.0, in1=cos_half[:], op0=ALU.mult, op1=ALU.mult
    )
    cos_less_one = consts.tile([P, ANGLES], F32)
    nc.vector.scalar_tensor_tensor(
        out=cos_less_one[:], in0=sin_half[:], scalar=-2.0, in1=sin_half[:], op0=ALU.mult, op1=ALU.mult
    )
    cos = consts.tile([P, ANGLES], F32)
    nc.vector.tensor_scalar(
        out=cos[:], in0=cos_less_one[:], scalar1=1.0, scalar2=None, op0=ALU.add
    )
    neg_cos = consts.tile([P, ANGLES], F32)
    nc.vector.tensor_scalar(
        out=neg_cos[:], in0=cos_less_one[:], scalar1=-1.0, scalar2=-1.0, op0=ALU.mult, op1=ALU.add
    )
    return cos, neg_cos, sin


def tile_attention_pa_t_kernel(tc, x, wq, wk, out_0, out_1):
    nc = tc.nc
    weights = (wq, wk)
    x_groups = x.flatten_outer_dims().rearrange(
        "(g p r) k -> g p (r k)", p=P, r=TILES_PER_GROUP
    )
    out_groups = [
        out.rearrange("b t h d -> (b t) (h d)").rearrange(
            "(g p r) c -> g p r c", p=P, r=TILES_PER_GROUP
        )
        for out in (out_0, out_1)
    ]

    with ExitStack() as stack:
        consts = stack.enter_context(tc.tile_pool(name="consts", bufs=1))
        x_pool = stack.enter_context(tc.tile_pool(name="x_pool", bufs=GROUPS))
        grouped_pool = stack.enter_context(tc.tile_pool(name="grouped_pool", bufs=3))
        quantised = stack.enter_context(tc.tile_pool(name="quantised", bufs=3))
        terms = stack.enter_context(tc.tile_pool(name="terms", bufs=4))
        results = stack.enter_context(tc.tile_pool(name="results", bufs=8))
        banks = stack.enter_context(tc.psum_pool(name="banks", bufs=PSUM_BANKS))
        stack.enter_context(tc.manual_schedule())

        w_raw = [consts.tile([P, 2 * 2 * CHANNELS], BF16, name="w_raw%d" % j) for j in range(2)]
        x_raw = [x_pool.tile([P, TILES_PER_GROUP * CHANNELS], BF16, name="x_raw") for g in range(GROUPS)]

        def load_weight(j):
            nc.sync.dma_start(
                out=w_raw[j][:].rearrange("p (h f) -> p h f", h=2),
                in_=weights[j].rearrange("(h p e) k -> p h (e k)", h=2, p=P, e=2),
            )

        load_weight(0)
        nc.sync.dma_start(out=x_raw[0][:], in_=x_groups[0])
        load_weight(1)
        for g in range(1, GROUPS):
            nc.sync.dma_start(out=x_raw[g][:], in_=x_groups[g])

        sin_half, cos_half = half_angle_sines(nc, consts)
        identity = consts.tile([P, P], F32)
        make_identity(nc, identity[:])

        def negate_odd_rows(j):
            odd_rows = w_raw[j][:].rearrange("p (h e k) -> p h e k", h=2, e=2)[:, :, 1, :]
            nc.vector.tensor_scalar(
                out=odd_rows, in0=odd_rows, scalar1=-1.0, scalar2=None, op0=ALU.mult
            )

        def transpose_words(words, starts):
            flipped = banks.tile([P, BANK], F32, tag="bank")
            for n, start in enumerate(starts):
                nc.tensor.transpose(
                    flipped[:, n * P : (n + 1) * P], words[:, start : start + P], identity[:]
                )
            return flipped

        def copy_second_bank(vector_helps, out, in_):
            if vector_helps:
                nc.vector.tensor_copy(out=out, in_=in_)
            else:
                nc.scalar.copy(out=out, in_=in_)

        def regroup_weight(j, vector_helps):
            words = w_raw[j][:].bitcast(F32)
            grouped = grouped_pool.tile([P, 4 * CHANNELS], BF16, align_bytes=64)
            halves = grouped[:].bitcast(F32).rearrange("p (n c u) -> p n c u", n=2, u=2)
            even = transpose_words(words, [(2 * h + 0) * WORDS + u * P for u in range(2) for h in range(2)])
            nc.scalar.copy(out=halves[:, 1, :, :], in_=even[:].rearrange("p (u c) -> p c u", u=2))
            odd = transpose_words(words, [(2 * h + 1) * WORDS + u * P for u in range(2) for h in range(2)])
            copy_second_bank(
                vector_helps, halves[:, 0, :, :], odd[:].rearrange("p (u c) -> p c u", u=2)
            )
            return grouped

        def regroup_tokens(g, vector_helps):
            words = x_raw[g][:].bitcast(F32)
            grouped = grouped_pool.tile([P, 4 * GROUP_TOKENS], BF16, align_bytes=64)
            halves = grouped[:].bitcast(F32).rearrange("p (n r c u) -> p n r c u", n=2, r=2, u=2)
            first = transpose_words(words, [r * WORDS + u * P for r in (0, 1) for u in range(2)])
            nc.scalar.copy(
                out=halves[:, 0, :, :, :], in_=first[:].rearrange("p (r u c) -> p r c u", r=2, u=2)
            )
            last = transpose_words(words, [r * WORDS + u * P for r in (2, 3) for u in range(2)])
            copy_second_bank(
                vector_helps, halves[:, 1, :, :, :], last[:].rearrange("p (r u c) -> p r c u", r=2, u=2)
            )
            return grouped

        def quantise(pool, name, grouped):
            codes = pool.tile([P, BANK], U32, name=name + "_codes", align_bytes=64)
            scales = pool.tile([P, BANK], U8, name=name + "_scales", align_bytes=64)
            nc.vector.quantize_mx(out=codes[:].bitcast(FP8X4), scales=scales[:], in_=grouped[:])
            return codes, scales

        def project_and_rotate(x_mx, w_mx, r, column, rotated):
            token_tile = slice(r * P, (r + 1) * P)
            product = banks.tile([P, BANK], F32, tag="bank")
            nc.tensor.matmul_mx(
                out=product[:],
                lhsT=x_mx[0][:, token_tile].bitcast(FP8X4),
                lhsT_scale=x_mx[1][:, token_tile],
                rhs=w_mx[0][:].bitcast(FP8X4),
                rhs_scale=w_mx[1][:],
                start=True,
                stop=True,
            )
            second = terms.tile([P, 2, PAIRS], F32)
            nc.scalar.activation(
                out=second[:, 0, :], in_=product[:, PAIRS:], func=ACT.Copy,
                scale=cos[:, column : column + 1],
            )
            nc.scalar.activation(
                out=second[:, 1, :], in_=product[:, :PAIRS], func=ACT.Copy,
                scale=neg_cos[:, column : column + 1],
            )
            nc.vector.scalar_tensor_tensor(
                out=rotated.rearrange("p (i e) -> p i e", e=2),
                in0=product[:].rearrange("p (e i) -> p i e", e=2),
                scalar=sin[:, column : column + 1],
                in1=second[:].rearrange("p e i -> p i e"),
                op0=ALU.mult,
                op1=ALU.add,
            )

        cos, neg_cos, sin = double_angles(nc, consts, sin_half, cos_half)
        negate_odd_rows(0)
        grouped_wq = regroup_weight(0, vector_helps=True)
        wq_mx = quantise(consts, "wq", grouped_wq)
        negate_odd_rows(1)
        grouped_x = regroup_tokens(0, vector_helps=False)
        next_x_mx = quantise(quantised, "x", grouped_x)
        grouped_wk = regroup_weight(1, vector_helps=False)
        wk_mx = quantise(consts, "wk", grouped_wk)
        w_mx = (wq_mx, wk_mx)

        for g in range(GROUPS):
            x_mx = next_x_mx
            last_group = g == GROUPS - 1
            made = 0
            for first_tile in range(0, TILES_PER_GROUP, TILES_PER_STORE):
                for j in range(2):
                    rotated = results.tile([P, TILES_PER_STORE, CHANNELS], F32)
                    for n in range(TILES_PER_STORE):
                        r = first_tile + n
                        if not last_group and made == REGROUP_AT:
                            grouped_x = regroup_tokens(g + 1, vector_helps=True)
                        if not last_group and made == REGROUP_AT + 1:
                            next_x_mx = quantise(quantised, "x", grouped_x)
                        column = (g % GROUPS_PER_SEQ) * TILES_PER_GROUP + r
                        project_and_rotate(x_mx, w_mx[j], r, column, rotated[:, n, :])
                        made += 1
                        if last_group:
                            nc.sync.dma_start(out=out_groups[j][g][:, r, :], in_=rotated[:, n, :])
                    if not last_group:
                        nc.sync.dma_start(
                            out=out_groups[j][g][:, first_tile : first_tile + TILES_PER_STORE, :],
                            in_=rotated[:],
                        )
